import numpy as np
import ml_dtypes


def mxq(x, axis, fmt="e4m3"):
    dtype, down = {"e4m3": (ml_dtypes.float8_e4m3fn, 7), "e5m2": (ml_dtypes.float8_e5m2, 14)}[fmt]
    v = np.moveaxis(np.asarray(x, np.float32).astype(ml_dtypes.bfloat16).astype(np.float64), axis, -1)
    blocks = v.reshape(v.shape[:-1] + (-1, 32))
    amax = np.abs(blocks).max(-1, keepdims=True)
    byte = np.maximum(np.where(amax > 0, np.frexp(amax)[1] - 1 + 127, 0) - down, 1)
    scale = np.exp2(byte - 127.0)
    codes = (blocks / scale).astype(np.float32).astype(dtype).astype(np.float64)
    return np.moveaxis((codes * scale).reshape(v.shape), -1, axis)


WIDE = False


def mx_kscale(k):
    if not WIDE:
        return np.ones(k)
    levels = np.array([10, -10, 5, -5, 0])
    a = np.random.permutation(np.resize(levels, k // 512 * 4)).reshape(k // 512, 4)
    idx = np.arange(k)
    return np.exp2(a[idx // 512, idx % 128 // 32])


BF16 = ml_dtypes.bfloat16


def bf(x):
    return np.asarray(x, np.float32).astype(BF16)


def f64(x):
    return np.asarray(x).astype(np.float64)


E2M1 = np.array([0.0, 0.5, 1.0, 1.5, 2.0, 3.0, 4.0, 6.0, -0.0, -0.5, -1.0, -1.5, -2.0, -3.0, -4.0, -6.0])


def pack_weight(w, fmt):
    k, n = w.shape
    w = f64(bf(w)).reshape(k // 32, 32, n)
    amax = np.abs(w).max(1)
    if fmt == "e4m3":
        byte = np.frexp(amax)[1] - 1 + 127 - 7
    else:
        mant, ex = np.frexp(amax / 6.0)
        byte = np.where(mant > 0.5, ex, ex - 1) + 127
    byte = np.clip(np.where(amax > 0, byte, 1), 1, 254)
    scaled = (w * np.exp2(127.0 - byte)[:, None, :]).reshape(k, n).astype(np.float32)
    by_word = np.ascontiguousarray(scaled.reshape(k // 512, 128, 4, n).transpose(0, 1, 3, 2))
    if fmt == "e4m3":
        words = by_word.astype(ml_dtypes.float8_e4m3fn).view(np.uint8)
    else:
        c = by_word.astype(ml_dtypes.float4_e2m1fn).view(np.uint8) & 0xF
        words = c[..., 0::2] | (c[..., 1::2] << 4)
    return np.ascontiguousarray(words), np.ascontiguousarray(byte.astype(np.uint8).reshape(k // 512, 16, n))


def unpack_weight(words, scales, fmt):
    g, p, n, _ = words.shape
    if fmt == "e4m3":
        vals = np.ascontiguousarray(words).view(ml_dtypes.float8_e4m3fn).astype(np.float64)
    else:
        nib = np.empty((g, p, n, 4), np.uint8)
        nib[..., 0::2] = words & 0xF
        nib[..., 1::2] = words >> 4
        vals = E2M1[nib]
    vals = vals * np.repeat(np.exp2(scales.astype(np.float64) - 127.0), 8, axis=1)[..., None]
    return vals.transpose(0, 1, 3, 2).reshape(g * 512, n)

def pack4(w):
    words, scales = pack_weight(w, "e2m1")
    return words.reshape(words.shape[0], 128, -1), scales


def unpack4(words, scales):
    return unpack_weight(words.reshape(words.shape[0], 128, -1, 2), scales, "e2m1")


N, IN, OUT = 1024, 2048, 2048


def setup_inputs():
    s = mx_kscale(IN)
    x = bf(np.random.standard_normal((N, IN)) * s)
    weight = np.random.standard_normal((OUT, IN)) * 0.02 / s[None, :]
    weight_words, weight_scales = pack4(np.ascontiguousarray(weight.T))
    bias = bf(np.random.standard_normal(OUT) * 0.5)
    input_scale = bf(np.ones(1))
    return {"x": x,
            "weight_words": weight_words,
            "weight_scales": weight_scales,
            "bias": bias,
            "input_scale": input_scale}


def reference(x, weight_words, weight_scales, bias, input_scale):
    xq = mxq(f64(x), 1, "e4m3")
    wt = unpack4(weight_words, weight_scales)
    return (xq @ wt) + f64(bias)

@@ -1,0 +1,201 @@
+from contextlib import ExitStack
+
+import concourse.bass as bass
+import concourse.mybir as mybir
+import concourse.tile as tile
+from concourse.masks import make_identity
+
+F32 = mybir.dt.float32
+BF16 = mybir.dt.bfloat16
+I32 = mybir.dt.int32
+U32 = mybir.dt.uint32
+U8 = mybir.dt.uint8
+FP8X4 = mybir.dt.float8_e4m3fn_x4
+FP4X4 = mybir.dt.float4_e2m1fn_x4
+ADD = mybir.AluOpType.add
+
+P = 128
+ROWS = 1024
+K = 2048
+N = 2048
+K_PASS = 512
+N_PASS = 512
+G = K // K_PASS
+NC = N // N_PASS
+MT = ROWS // P
+FLOPS = 2 * ROWS * K * N
+
+SORT_FROM = 99
+
+
+def tile_inputscaledquantlinear_kernel(tc, x, weight_words, weight_scales, bias, input_scale, out):
+    nc = tc.nc
+    with ExitStack() as ctx:
+        keep = ctx.enter_context(tc.tile_pool(name="keep", bufs=1))
+        work = ctx.enter_context(tc.tile_pool(name="work", bufs=3))
+        outp = ctx.enter_context(tc.tile_pool(name="outp", bufs=4))
+        psum = ctx.enter_context(tc.psum_pool(name="psum", bufs=1))
+        ctx.enter_context(tc.manual_schedule())
+
+        ident = keep.tile([P, P], F32, name="ident")
+        ones = keep.tile([P, P], BF16, name="ones")
+        brow = keep.tile([P, N], BF16, name="brow")
+        bias_sb = keep.tile([P, N], F32, name="bias_sb")
+        w_sb = [keep.tile([P, 2 * N], U8, name="w%d" % g, align_bytes=64) for g in range(G)]
+        wsc = [keep.tile([P, 2, N], U8, name="wsc%d" % h, align_bytes=64) for h in range(2)]
+        x_sb = [keep.tile([P, K], BF16, name="x%d" % i) for i in range(MT)]
+        xq = [keep.tile([P, K // 4], U32, name="xq%d" % i, align_bytes=64) for i in range(MT)]
+        xsc = [keep.tile([P, K // 4], U8, name="xsc%d" % i, align_bytes=64) for i in range(MT)]
+
+        count = [0]
+
+        def new_bank():
+            b = count[0] % 8
+            count[0] += 1
+            return psum.tile([P, 512], F32, tag="bank%d" % b, name="ps%d" % count[0])
+
+        def load_x(i):
+            nc.sync.dma_start(out=x_sb[i][:], in_=x[P * i : P * (i + 1), :])
+
+        def load_w(g):
+            nc.sync.dma_start(out=w_sb[g][:].bitcast(I32), in_=weight_words[g].bitcast(I32))
+
+        def load_scales(h):
+            for r in range(4):
+                nc.sync.dma_start(
+                    out=wsc[h][r:P:32, :, :].bitcast(I32),
+                    in_=weight_scales[2 * h : 2 * h + 2, r:16:4, :].rearrange("g q n -> q g n").bitcast(I32),
+                )
+
+        grouped = {}
+
+        def transposes(i):
+            words = x_sb[i][:].bitcast(F32)
+            if i >= SORT_FROM:
+                srt = work.tile([P, K // 2], F32, name="srt")
+                nc.scalar.copy(
+                    out=srt[:].rearrange("p (g u q) -> p g u q", g=G, u=2),
+                    in_=words.rearrange("p (g q u) -> p g u q", g=G, u=2),
+                )
+            grp = work.tile([P, K], BF16, name="grp", align_bytes=64)
+            grouped[i] = grp
+            banks = []
+            for h in range(2):
+                bank = new_bank()
+                banks.append(bank)
+                for s in range(4):
+                    g = 2 * h + s // 2
+                    u = s % 2
+                    if i >= SORT_FROM:
+                        src = srt[:, P * (2 * g + u) : P * (2 * g + u + 1)]
+                    else:
+                        src = words[:, 256 * g + u : 256 * (g + 1) : 2]
+                    nc.tensor.transpose(bank[:, P * s : P * (s + 1)], src, ident[:])
+            for h in range(2):
+                nc.scalar.copy(
+                    out=grp[:].bitcast(F32)[:, 512 * h : 512 * (h + 1)].rearrange("p (g m u) -> p g m u", g=2, u=2),
+                    in_=banks[h][:].rearrange("p (g u m) -> p g m u", g=2, u=2),
+                )
+
+        def quantise(i):
+            for h in range(2):
+                nc.vector.quantize_mx(
+                    out=xq[i][:, 256 * h : 256 * (h + 1)].bitcast(FP8X4),
+                    scales=xsc[i][:, 256 * h : 256 * (h + 1)],
+                    in_=grouped[i][:, 1024 * h : 1024 * (h + 1)],
+                )
+
+        def mx_pass(acc, i, n, g):
+            nc.tensor.matmul_mx(
+                out=acc[:],
+                lhsT=xq[i][:, P * g : P * (g + 1)].bitcast(FP8X4),
+                lhsT_scale=xsc[i][:, P * g : P * (g + 1)],
+                rhs=w_sb[g][:, 1024 * n : 1024 * (n + 1)].bitcast(FP4X4),
+                rhs_scale=wsc[g // 2][:, g % 2, N_PASS * n : N_PASS * (n + 1)],
+                start=(g == 0),
+                stop=(g == G - 1),
+            )
+
+        accs = {}
+        res = {}
+
+        def group(i, n):
+            accs[(i, n)] = new_bank()
+            for g in range(G):
+                mx_pass(accs[(i, n)], i, n, g)
+
+        def drain(i, n, store_from):
+            if n == 0:
+                res[i] = outp.tile([P, N], F32, name="res")
+            cols = slice(N_PASS * n, N_PASS * (n + 1))
+            nc.vector.tensor_tensor(out=res[i][:, cols], in0=accs[(i, n)][:], in1=bias_sb[:, cols], op=ADD)
+            if store_from is not None:
+                c = slice(N_PASS * store_from, N_PASS * (n + 1))
+                nc.sync.dma_start(out=out[P * i : P * (i + 1), c], in_=res[i][:, c])
+
+        nc.vector.memset(brow[:].bitcast(I32), 0)
+        nc.scalar.dma_start(out=brow[0:1, :], in_=bias.rearrange("(o n) -> o n", o=1))
+        nc.vector.memset(wsc[0][:].rearrange("p g n -> p (g n)").bitcast(I32), 0)
+        nc.vector.memset(ones[:], 1.0)
+        nc.vector.memset(wsc[1][:].rearrange("p g n -> p (g n)").bitcast(I32), 0)
+        make_identity(nc, ident[:])
+        load_x(0)
+        load_x(1)
+        load_scales(0)
+        load_w(0)
+        load_w(1)
+        load_scales(1)
+        load_w(2)
+        load_w(3)
+        for i in range(2, MT):
+            load_x(i)
+
+        transposes(0)
+        quantise(0)
+        transposes(1)
+        quantise(1)
+
+        bb = []
+        for n in range(NC):
+            bank = new_bank()
+            bb.append(bank)
+            nc.tensor.matmul(out=bank[:], lhsT=ones[:], rhs=brow[:, N_PASS * n : N_PASS * (n + 1)], start=True, stop=True)
+        for n in range(NC):
+            cols = slice(N_PASS * n, N_PASS * (n + 1))
+            if n < 2:
+                nc.scalar.copy(out=bias_sb[:, cols], in_=bb[n][:])
+            else:
+                nc.vector.tensor_copy(out=bias_sb[:, cols], in_=bb[n][:])
+
+        head = [(0, 0), (0, 1), (0, 2), (0, 3), (1, 0), (1, 1)]
+        for (i, n) in head:
+            accs[(i, n)] = new_bank()
+        for g in range(G):
+            for (i, n) in head:
+                mx_pass(accs[(i, n)], i, n, g)
+        transposes(2)
+        drain(0, 0, None)
+        drain(0, 1, 0)
+        drain(0, 2, None)
+        drain(0, 3, 2)
+        drain(1, 0, None)
+        drain(1, 1, 0)
+        quantise(2)
+        group(1, 2)
+        group(1, 3)
+        transposes(3)
+        drain(1, 2, None)
+        drain(1, 3, 2)
+        quantise(3)
+        for i in range(2, MT):
+            for n in range(NC):
+                group(i, n)
+            if i + 2 < MT:
+                transposes(i + 2)
+            last = i == MT - 1
+            drain(i, 0, 0 if last else None)
+            drain(i, 1, 1 if last else 0)
+            drain(i, 2, 2 if last else None)
+            drain(i, 3, 3 if last else 2)
+            if i + 2 < MT:
+                quantise(i + 2)

@@ -25,7 +25,7 @@ NC = N // N_PASS
 MT = ROWS // P
 FLOPS = 2 * ROWS * K * N
 
-SORT_FROM = 99
+SORT_FROM = 2
 
 
 def tile_inputscaledquantlinear_kernel(tc, x, weight_words, weight_scales, bias, input_scale, out):
@@ -176,26 +176,29 @@ def tile_inputscaledquantlinear_kernel(tc, x, weight_words, weight_scales, bias,
         transposes(2)
         drain(0, 0, None)
         drain(0, 1, 0)
+        transposes(3)
         drain(0, 2, None)
         drain(0, 3, 2)
         drain(1, 0, None)
-        drain(1, 1, 0)
         quantise(2)
+        drain(1, 1, 0)
+        quantise(3)
         group(1, 2)
         group(1, 3)
-        transposes(3)
         drain(1, 2, None)
         drain(1, 3, 2)
-        quantise(3)
         for i in range(2, MT):
             for n in range(NC):
                 group(i, n)
-            if i + 2 < MT:
+            pair = i % 2 == 0 and i + 3 < MT
+            if pair:
                 transposes(i + 2)
+                transposes(i + 3)
             last = i == MT - 1
             drain(i, 0, 0 if last else None)
             drain(i, 1, 1 if last else 0)
             drain(i, 2, 2 if last else None)
             drain(i, 3, 3 if last else 2)
-            if i + 2 < MT:
+            if pair:
                 quantise(i + 2)
+                quantise(i + 3)

@@ -33,6 +33,7 @@ def tile_inputscaledquantlinear_kernel(tc, x, weight_words, weight_scales, bias,
     with ExitStack() as ctx:
         keep = ctx.enter_context(tc.tile_pool(name="keep", bufs=1))
         work = ctx.enter_context(tc.tile_pool(name="work", bufs=3))
+        srtp = ctx.enter_context(tc.tile_pool(name="srtp", bufs=4))
         outp = ctx.enter_context(tc.tile_pool(name="outp", bufs=4))
         psum = ctx.enter_context(tc.psum_pool(name="psum", bufs=1))
         ctx.enter_context(tc.manual_schedule())
@@ -68,15 +69,20 @@ def tile_inputscaledquantlinear_kernel(tc, x, weight_words, weight_scales, bias,
                 )
 
         grouped = {}
+        sorted_x = {}
+
+        def sort_words(i):
+            srt = srtp.tile([P, K // 2], F32, name="srt")
+            sorted_x[i] = srt
+            nc.scalar.copy(
+                out=srt[:].rearrange("p (g u q) -> p g u q", g=G, u=2),
+                in_=x_sb[i][:].bitcast(F32).rearrange("p (g q u) -> p g u q", g=G, u=2),
+            )
 
         def transposes(i):
             words = x_sb[i][:].bitcast(F32)
             if i >= SORT_FROM:
-                srt = work.tile([P, K // 2], F32, name="srt")
-                nc.scalar.copy(
-                    out=srt[:].rearrange("p (g u q) -> p g u q", g=G, u=2),
-                    in_=words.rearrange("p (g q u) -> p g u q", g=G, u=2),
-                )
+                srt = sorted_x[i]
             grp = work.tile([P, K], BF16, name="grp", align_bytes=64)
             grouped[i] = grp
             banks = []
@@ -167,6 +173,9 @@ def tile_inputscaledquantlinear_kernel(tc, x, weight_words, weight_scales, bias,
             else:
                 nc.vector.tensor_copy(out=bias_sb[:, cols], in_=bb[n][:])
 
+        sort_words(2)
+        sort_words(3)
+
         head = [(0, 0), (0, 1), (0, 2), (0, 3), (1, 0), (1, 1)]
         for (i, n) in head:
             accs[(i, n)] = new_bank()
@@ -177,6 +186,8 @@ def tile_inputscaledquantlinear_kernel(tc, x, weight_words, weight_scales, bias,
         drain(0, 0, None)
         drain(0, 1, 0)
         transposes(3)
+        sort_words(4)
+        sort_words(5)
         drain(0, 2, None)
         drain(0, 3, 2)
         drain(1, 0, None)
@@ -194,6 +205,9 @@ def tile_inputscaledquantlinear_kernel(tc, x, weight_words, weight_scales, bias,
             if pair:
                 transposes(i + 2)
                 transposes(i + 3)
+                if i + 5 < MT:
+                    sort_words(i + 4)
+                    sort_words(i + 5)
             last = i == MT - 1
             drain(i, 0, 0 if last else None)
             drain(i, 1, 1 if last else 0)

@@ -25,7 +25,8 @@ NC = N // N_PASS
 MT = ROWS // P
 FLOPS = 2 * ROWS * K * N
 
-SORT_FROM = 2
+SORT_FROM = 4
+WARM = 5
 
 
 def tile_inputscaledquantlinear_kernel(tc, x, weight_words, weight_scales, bias, input_scale, out):
@@ -41,6 +42,7 @@ def tile_inputscaledquantlinear_kernel(tc, x, weight_words, weight_scales, bias,
         ident = keep.tile([P, P], F32, name="ident")
         ones = keep.tile([P, P], BF16, name="ones")
         brow = keep.tile([P, N], BF16, name="brow")
+        zeros = keep.tile([P, N_PASS], BF16, name="zeros")
         bias_sb = keep.tile([P, N], F32, name="bias_sb")
         w_sb = [keep.tile([P, 2 * N], U8, name="w%d" % g, align_bytes=64) for g in range(G)]
         wsc = [keep.tile([P, 2, N], U8, name="wsc%d" % h, align_bytes=64) for h in range(2)]
@@ -139,10 +141,11 @@ def tile_inputscaledquantlinear_kernel(tc, x, weight_words, weight_scales, bias,
                 c = slice(N_PASS * store_from, N_PASS * (n + 1))
                 nc.sync.dma_start(out=out[P * i : P * (i + 1), c], in_=res[i][:, c])
 
+        nc.vector.memset(ones[:], 1.0)
+        nc.vector.memset(zeros[:].bitcast(I32), 0)
         nc.vector.memset(brow[:].bitcast(I32), 0)
         nc.scalar.dma_start(out=brow[0:1, :], in_=bias.rearrange("(o n) -> o n", o=1))
         nc.vector.memset(wsc[0][:].rearrange("p g n -> p (g n)").bitcast(I32), 0)
-        nc.vector.memset(ones[:], 1.0)
         nc.vector.memset(wsc[1][:].rearrange("p g n -> p (g n)").bitcast(I32), 0)
         make_identity(nc, ident[:])
         load_x(0)
@@ -155,6 +158,10 @@ def tile_inputscaledquantlinear_kernel(tc, x, weight_words, weight_scales, bias,
         load_w(3)
         for i in range(2, MT):
             load_x(i)
+
+        warm = psum.tile([P, 512], F32, tag="bank7", name="warm")
+        for d in range(WARM):
+            nc.tensor.matmul(out=warm[:], lhsT=ones[:], rhs=zeros[:], start=True, stop=True)
 
         transposes(0)
         quantise(0)
@@ -172,9 +179,6 @@ def tile_inputscaledquantlinear_kernel(tc, x, weight_words, weight_scales, bias,
                 nc.scalar.copy(out=bias_sb[:, cols], in_=bb[n][:])
             else:
                 nc.vector.tensor_copy(out=bias_sb[:, cols], in_=bb[n][:])
-
-        sort_words(2)
-        sort_words(3)
 
         head = [(0, 0), (0, 1), (0, 2), (0, 3), (1, 0), (1, 1)]
         for (i, n) in head:

@@ -1,8 +1,6 @@
 from contextlib import ExitStack
 
-import concourse.bass as bass
 import concourse.mybir as mybir
-import concourse.tile as tile
 from concourse.masks import make_identity
 
 F32 = mybir.dt.float32
@@ -26,7 +24,8 @@ MT = ROWS // P
 FLOPS = 2 * ROWS * K * N
 
 SORT_FROM = 4
-WARM = 5
+WARM = 4
+TAPER = 4
 
 
 def tile_inputscaledquantlinear_kernel(tc, x, weight_words, weight_scales, bias, input_scale, out):
@@ -34,16 +33,16 @@ def tile_inputscaledquantlinear_kernel(tc, x, weight_words, weight_scales, bias,
     with ExitStack() as ctx:
         keep = ctx.enter_context(tc.tile_pool(name="keep", bufs=1))
         work = ctx.enter_context(tc.tile_pool(name="work", bufs=3))
-        srtp = ctx.enter_context(tc.tile_pool(name="srtp", bufs=4))
+        srtp = ctx.enter_context(tc.tile_pool(name="srtp", bufs=3))
         outp = ctx.enter_context(tc.tile_pool(name="outp", bufs=4))
         psum = ctx.enter_context(tc.psum_pool(name="psum", bufs=1))
         ctx.enter_context(tc.manual_schedule())
 
         ident = keep.tile([P, P], F32, name="ident")
         ones = keep.tile([P, P], BF16, name="ones")
-        brow = keep.tile([P, N], BF16, name="brow")
         zeros = keep.tile([P, N_PASS], BF16, name="zeros")
-        bias_sb = keep.tile([P, N], F32, name="bias_sb")
+        brow = keep.tile([P, N], BF16, name="brow")
+        bias_sb = keep.tile([P, N], BF16, name="bias_sb")
         w_sb = [keep.tile([P, 2 * N], U8, name="w%d" % g, align_bytes=64) for g in range(G)]
         wsc = [keep.tile([P, 2, N], U8, name="wsc%d" % h, align_bytes=64) for h in range(2)]
         x_sb = [keep.tile([P, K], BF16, name="x%d" % i) for i in range(MT)]
@@ -52,16 +51,22 @@ def tile_inputscaledquantlinear_kernel(tc, x, weight_words, weight_scales, bias,
 
         count = [0]
 
-        def new_bank():
+        def new_bank(shape, dtype):
             b = count[0] % 8
             count[0] += 1
-            return psum.tile([P, 512], F32, tag="bank%d" % b, name="ps%d" % count[0])
+            return psum.tile(shape, dtype, tag="bank%d" % b, name="ps%d" % count[0])
 
-        def load_x(i):
-            nc.sync.dma_start(out=x_sb[i][:], in_=x[P * i : P * (i + 1), :])
+        def load_x(i, pieces):
+            step = K // pieces
+            for c in range(pieces):
+                cols = slice(step * c, step * (c + 1))
+                nc.sync.dma_start(out=x_sb[i][:, cols], in_=x[P * i : P * (i + 1), cols])
 
-        def load_w(g):
-            nc.sync.dma_start(out=w_sb[g][:].bitcast(I32), in_=weight_words[g].bitcast(I32))
+        def load_w(g, pieces):
+            step = 2 * N // pieces
+            for c in range(pieces):
+                cols = slice(step * c, step * (c + 1))
+                nc.sync.dma_start(out=w_sb[g][:, cols].bitcast(I32), in_=weight_words[g][:, cols].bitcast(I32))
 
         def load_scales(h):
             for r in range(4):
@@ -83,19 +88,17 @@ def tile_inputscaledquantlinear_kernel(tc, x, weight_words, weight_scales, bias,
 
         def transposes(i):
             words = x_sb[i][:].bitcast(F32)
-            if i >= SORT_FROM:
-                srt = sorted_x[i]
             grp = work.tile([P, K], BF16, name="grp", align_bytes=64)
             grouped[i] = grp
             banks = []
             for h in range(2):
-                bank = new_bank()
+                bank = new_bank([P, 512], F32)
                 banks.append(bank)
                 for s in range(4):
                     g = 2 * h + s // 2
                     u = s % 2
                     if i >= SORT_FROM:
-                        src = srt[:, P * (2 * g + u) : P * (2 * g + u + 1)]
+                        src = sorted_x[i][:, P * (2 * g + u) : P * (2 * g + u + 1)]
                     else:
                         src = words[:, 256 * g + u : 256 * (g + 1) : 2]
                     nc.tensor.transpose(bank[:, P * s : P * (s + 1)], src, ident[:])
@@ -113,13 +116,13 @@ def tile_inputscaledquantlinear_kernel(tc, x, weight_words, weight_scales, bias,
                     in_=grouped[i][:, 1024 * h : 1024 * (h + 1)],
                 )
 
-        def mx_pass(acc, i, n, g):
+        def mx_pass(acc, i, c0, width, g):
             nc.tensor.matmul_mx(
-                out=acc[:],
+                out=acc[:, 0:width],
                 lhsT=xq[i][:, P * g : P * (g + 1)].bitcast(FP8X4),
                 lhsT_scale=xsc[i][:, P * g : P * (g + 1)],
-                rhs=w_sb[g][:, 1024 * n : 1024 * (n + 1)].bitcast(FP4X4),
-                rhs_scale=wsc[g // 2][:, g % 2, N_PASS * n : N_PASS * (n + 1)],
+                rhs=w_sb[g][:, 2 * c0 : 2 * (c0 + width)].bitcast(FP4X4),
+                rhs_scale=wsc[g // 2][:, g % 2, c0 : c0 + width],
                 start=(g == 0),
                 stop=(g == G - 1),
             )
@@ -127,18 +130,18 @@ def tile_inputscaledquantlinear_kernel(tc, x, weight_words, weight_scales, bias,
         accs = {}
         res = {}
 
-        def group(i, n):
-            accs[(i, n)] = new_bank()
+        def group(i, c0, width):
+            accs[(i, c0)] = new_bank([P, 512], F32)
             for g in range(G):
-                mx_pass(accs[(i, n)], i, n, g)
+                mx_pass(accs[(i, c0)], i, c0, width, g)
 
-        def drain(i, n, store_from):
-            if n == 0:
+        def drain(i, c0, width, store_from):
+            if c0 == 0:
                 res[i] = outp.tile([P, N], F32, name="res")
-            cols = slice(N_PASS * n, N_PASS * (n + 1))
-            nc.vector.tensor_tensor(out=res[i][:, cols], in0=accs[(i, n)][:], in1=bias_sb[:, cols], op=ADD)
+            cols = slice(c0, c0 + width)
+            nc.vector.tensor_tensor(out=res[i][:, cols], in0=accs[(i, c0)][:, 0:width], in1=bias_sb[:, cols], op=ADD)
             if store_from is not None:
-                c = slice(N_PASS * store_from, N_PASS * (n + 1))
+                c = slice(store_from, c0 + width)
                 nc.sync.dma_start(out=out[P * i : P * (i + 1), c], in_=res[i][:, c])
 
         nc.vector.memset(ones[:], 1.0)
@@ -148,16 +151,16 @@ def tile_inputscaledquantlinear_kernel(tc, x, weight_words, weight_scales, bias,
         nc.vector.memset(wsc[0][:].rearrange("p g n -> p (g n)").bitcast(I32), 0)
         nc.vector.memset(wsc[1][:].rearrange("p g n -> p (g n)").bitcast(I32), 0)
         make_identity(nc, ident[:])
-        load_x(0)
-        load_x(1)
+        load_x(0, 2)
+        load_x(1, 1)
         load_scales(0)
-        load_w(0)
-        load_w(1)
+        load_w(0, 2)
+        load_w(1, 1)
         load_scales(1)
-        load_w(2)
-        load_w(3)
+        load_w(2, 1)
+        load_w(3, 1)
         for i in range(2, MT):
-            load_x(i)
+            load_x(i, 1)
 
         warm = psum.tile([P, 512], F32, tag="bank7", name="warm")
         for d in range(WARM):
@@ -165,58 +168,62 @@ def tile_inputscaledquantlinear_kernel(tc, x, weight_words, weight_scales, bias,
 
         transposes(0)
         quantise(0)
+
+        for h in range(2):
+            bank = new_bank([P, 1024], BF16)
+            for c in range(2):
+                nc.tensor.matmul(
+                    out=bank[:, 512 * c : 512 * (c + 1)],
+                    lhsT=ones[:],
+                    rhs=brow[:, 1024 * h + 512 * c : 1024 * h + 512 * (c + 1)],
+                    start=True,
+                    stop=True,
+                )
+            if h == 0:
+                nc.scalar.copy(out=bias_sb[:, 0:1024], in_=bank[:])
+            else:
+                nc.vector.tensor_copy(out=bias_sb[:, 1024:2048], in_=bank[:])
+
         transposes(1)
         quantise(1)
 
-        bb = []
-        for n in range(NC):
-            bank = new_bank()
-            bb.append(bank)
-            nc.tensor.matmul(out=bank[:], lhsT=ones[:], rhs=brow[:, N_PASS * n : N_PASS * (n + 1)], start=True, stop=True)
-        for n in range(NC):
-            cols = slice(N_PASS * n, N_PASS * (n + 1))
-            if n < 2:
-                nc.scalar.copy(out=bias_sb[:, cols], in_=bb[n][:])
-            else:
-                nc.vector.tensor_copy(out=bias_sb[:, cols], in_=bb[n][:])
-
-        head = [(0, 0), (0, 1), (0, 2), (0, 3), (1, 0), (1, 1)]
-        for (i, n) in head:
-            accs[(i, n)] = new_bank()
+        head = [(0, 0), (0, 512), (0, 1024), (0, 1536), (1, 0), (1, 512)]
+        for (i, c0) in head:
+            accs[(i, c0)] = new_bank([P, 512], F32)
         for g in range(G):
-            for (i, n) in head:
-                mx_pass(accs[(i, n)], i, n, g)
+            for (i, c0) in head:
+                mx_pass(accs[(i, c0)], i, c0, N_PASS, g)
         transposes(2)
-        drain(0, 0, None)
-        drain(0, 1, 0)
+        drain(0, 0, 512, None)
+        drain(0, 512, 512, 0)
+        drain(0, 1024, 512, None)
+        drain(0, 1536, 512, 1024)
+        drain(1, 0, 512, None)
+        drain(1, 512, 512, 0)
+        quantise(2)
+        group(1, 1024, 512)
+        group(1, 1536, 512)
         transposes(3)
         sort_words(4)
-        sort_words(5)
-        drain(0, 2, None)
-        drain(0, 3, 2)
-        drain(1, 0, None)
-        quantise(2)
-        drain(1, 1, 0)
+        drain(1, 1024, 512, None)
+        drain(1, 1536, 512, 1024)
         quantise(3)
-        group(1, 2)
-        group(1, 3)
-        drain(1, 2, None)
-        drain(1, 3, 2)
         for i in range(2, MT):
-            for n in range(NC):
-                group(i, n)
-            pair = i % 2 == 0 and i + 3 < MT
-            if pair:
-                transposes(i + 2)
-                transposes(i + 3)
-                if i + 5 < MT:
-                    sort_words(i + 4)
-                    sort_words(i + 5)
             last = i == MT - 1
-            drain(i, 0, 0 if last else None)
-            drain(i, 1, 1 if last else 0)
-            drain(i, 2, 2 if last else None)
-            drain(i, 3, 3 if last else 2)
-            if pair:
+            pieces = [(0, 512), (512, 512), (1024, 512), (1536, 512)]
+            if last:
+                step = 512 // TAPER
+                pieces = pieces[0:3] + [(1536 + step * s, step) for s in range(TAPER)]
+            for (c0, width) in pieces:
+                group(i, c0, width)
+            if i + 2 < MT:
+                transposes(i + 2)
+            if i + 3 < MT:
+                sort_words(i + 3)
+            for j, (c0, width) in enumerate(pieces):
+                if last:
+                    drain(i, c0, width, c0)
+                else:
+                    drain(i, c0, width, c0 - 512 if j % 2 == 1 else None)
+            if i + 2 < MT:
                 quantise(i + 2)
-                quantise(i + 3)

@@ -23,8 +23,6 @@ NC = N // N_PASS
 MT = ROWS // P
 FLOPS = 2 * ROWS * K * N
 
-SORT_FROM = 4
-WARM = 4
 TAPER = 4
 
 
@@ -33,14 +31,12 @@ def tile_inputscaledquantlinear_kernel(tc, x, weight_words, weight_scales, bias,
     with ExitStack() as ctx:
         keep = ctx.enter_context(tc.tile_pool(name="keep", bufs=1))
         work = ctx.enter_context(tc.tile_pool(name="work", bufs=3))
-        srtp = ctx.enter_context(tc.tile_pool(name="srtp", bufs=3))
         outp = ctx.enter_context(tc.tile_pool(name="outp", bufs=4))
         psum = ctx.enter_context(tc.psum_pool(name="psum", bufs=1))
         ctx.enter_context(tc.manual_schedule())
 
         ident = keep.tile([P, P], F32, name="ident")
         ones = keep.tile([P, P], BF16, name="ones")
-        zeros = keep.tile([P, N_PASS], BF16, name="zeros")
         brow = keep.tile([P, N], BF16, name="brow")
         bias_sb = keep.tile([P, N], BF16, name="bias_sb")
         w_sb = [keep.tile([P, 2 * N], U8, name="w%d" % g, align_bytes=64) for g in range(G)]
@@ -76,15 +72,6 @@ def tile_inputscaledquantlinear_kernel(tc, x, weight_words, weight_scales, bias,
                 )
 
         grouped = {}
-        sorted_x = {}
-
-        def sort_words(i):
-            srt = srtp.tile([P, K // 2], F32, name="srt")
-            sorted_x[i] = srt
-            nc.scalar.copy(
-                out=srt[:].rearrange("p (g u q) -> p g u q", g=G, u=2),
-                in_=x_sb[i][:].bitcast(F32).rearrange("p (g q u) -> p g u q", g=G, u=2),
-            )
 
         def transposes(i):
             words = x_sb[i][:].bitcast(F32)
@@ -97,10 +84,7 @@ def tile_inputscaledquantlinear_kernel(tc, x, weight_words, weight_scales, bias,
                 for s in range(4):
                     g = 2 * h + s // 2
                     u = s % 2
-                    if i >= SORT_FROM:
-                        src = sorted_x[i][:, P * (2 * g + u) : P * (2 * g + u + 1)]
-                    else:
-                        src = words[:, 256 * g + u : 256 * (g + 1) : 2]
+                    src = words[:, 256 * g + u : 256 * (g + 1) : 2]
                     nc.tensor.transpose(bank[:, P * s : P * (s + 1)], src, ident[:])
             for h in range(2):
                 nc.scalar.copy(
@@ -145,7 +129,6 @@ def tile_inputscaledquantlinear_kernel(tc, x, weight_words, weight_scales, bias,
                 nc.sync.dma_start(out=out[P * i : P * (i + 1), c], in_=res[i][:, c])
 
         nc.vector.memset(ones[:], 1.0)
-        nc.vector.memset(zeros[:].bitcast(I32), 0)
         nc.vector.memset(brow[:].bitcast(I32), 0)
         nc.scalar.dma_start(out=brow[0:1, :], in_=bias.rearrange("(o n) -> o n", o=1))
         nc.vector.memset(wsc[0][:].rearrange("p g n -> p (g n)").bitcast(I32), 0)
@@ -161,10 +144,6 @@ def tile_inputscaledquantlinear_kernel(tc, x, weight_words, weight_scales, bias,
         load_w(3, 1)
         for i in range(2, MT):
             load_x(i, 1)
-
-        warm = psum.tile([P, 512], F32, tag="bank7", name="warm")
-        for d in range(WARM):
-            nc.tensor.matmul(out=warm[:], lhsT=ones[:], rhs=zeros[:], start=True, stop=True)
 
         transposes(0)
         quantise(0)
@@ -204,7 +183,6 @@ def tile_inputscaledquantlinear_kernel(tc, x, weight_words, weight_scales, bias,
         group(1, 1024, 512)
         group(1, 1536, 512)
         transposes(3)
-        sort_words(4)
         drain(1, 1024, 512, None)
         drain(1, 1536, 512, 1024)
         quantise(3)
@@ -218,8 +196,6 @@ def tile_inputscaledquantlinear_kernel(tc, x, weight_words, weight_scales, bias,
                 group(i, c0, width)
             if i + 2 < MT:
                 transposes(i + 2)
-            if i + 3 < MT:
-                sort_words(i + 3)
             for j, (c0, width) in enumerate(pieces):
                 if last:
                     drain(i, c0, width, c0)

@@ -23,6 +23,8 @@ NC = N // N_PASS
 MT = ROWS // P
 FLOPS = 2 * ROWS * K * N
 
+SORT_FROM = 4
+WARM = 4
 TAPER = 4
 
 
@@ -31,12 +33,14 @@ def tile_inputscaledquantlinear_kernel(tc, x, weight_words, weight_scales, bias,
     with ExitStack() as ctx:
         keep = ctx.enter_context(tc.tile_pool(name="keep", bufs=1))
         work = ctx.enter_context(tc.tile_pool(name="work", bufs=3))
+        srtp = ctx.enter_context(tc.tile_pool(name="srtp", bufs=3))
         outp = ctx.enter_context(tc.tile_pool(name="outp", bufs=4))
         psum = ctx.enter_context(tc.psum_pool(name="psum", bufs=1))
         ctx.enter_context(tc.manual_schedule())
 
         ident = keep.tile([P, P], F32, name="ident")
         ones = keep.tile([P, P], BF16, name="ones")
+        zeros = keep.tile([P, N_PASS], BF16, name="zeros")
         brow = keep.tile([P, N], BF16, name="brow")
         bias_sb = keep.tile([P, N], BF16, name="bias_sb")
         w_sb = [keep.tile([P, 2 * N], U8, name="w%d" % g, align_bytes=64) for g in range(G)]
@@ -72,28 +76,41 @@ def tile_inputscaledquantlinear_kernel(tc, x, weight_words, weight_scales, bias,
                 )
 
         grouped = {}
+        sorted_x = {}
 
-        def transposes(i):
+        def sort_words(i):
+            srt = srtp.tile([P, K // 2], F32, name="srt")
+            sorted_x[i] = srt
+            nc.scalar.copy(
+                out=srt[:].rearrange("p (g u q) -> p g u q", g=G, u=2),
+                in_=x_sb[i][:].bitcast(F32).rearrange("p (g q u) -> p g u q", g=G, u=2),
+            )
+
+        def transposes(i, halves):
             words = x_sb[i][:].bitcast(F32)
-            grp = work.tile([P, K], BF16, name="grp", align_bytes=64)
-            grouped[i] = grp
-            banks = []
-            for h in range(2):
+            if halves[0] == 0:
+                grouped[i] = work.tile([P, K], BF16, name="grp", align_bytes=64)
+            grp = grouped[i]
+            banks = {}
+            for h in halves:
                 bank = new_bank([P, 512], F32)
-                banks.append(bank)
+                banks[h] = bank
                 for s in range(4):
                     g = 2 * h + s // 2
                     u = s % 2
-                    src = words[:, 256 * g + u : 256 * (g + 1) : 2]
+                    if i >= SORT_FROM:
+                        src = sorted_x[i][:, P * (2 * g + u) : P * (2 * g + u + 1)]
+                    else:
+                        src = words[:, 256 * g + u : 256 * (g + 1) : 2]
                     nc.tensor.transpose(bank[:, P * s : P * (s + 1)], src, ident[:])
-            for h in range(2):
+            for h in halves:
                 nc.scalar.copy(
                     out=grp[:].bitcast(F32)[:, 512 * h : 512 * (h + 1)].rearrange("p (g m u) -> p g m u", g=2, u=2),
                     in_=banks[h][:].rearrange("p (g u m) -> p g m u", g=2, u=2),
                 )
 
-        def quantise(i):
-            for h in range(2):
+        def quantise(i, halves):
+            for h in halves:
                 nc.vector.quantize_mx(
                     out=xq[i][:, 256 * h : 256 * (h + 1)].bitcast(FP8X4),
                     scales=xsc[i][:, 256 * h : 256 * (h + 1)],
@@ -129,6 +146,7 @@ def tile_inputscaledquantlinear_kernel(tc, x, weight_words, weight_scales, bias,
                 nc.sync.dma_start(out=out[P * i : P * (i + 1), c], in_=res[i][:, c])
 
         nc.vector.memset(ones[:], 1.0)
+        nc.vector.memset(zeros[:].bitcast(I32), 0)
         nc.vector.memset(brow[:].bitcast(I32), 0)
         nc.scalar.dma_start(out=brow[0:1, :], in_=bias.rearrange("(o n) -> o n", o=1))
         nc.vector.memset(wsc[0][:].rearrange("p g n -> p (g n)").bitcast(I32), 0)
@@ -145,8 +163,12 @@ def tile_inputscaledquantlinear_kernel(tc, x, weight_words, weight_scales, bias,
         for i in range(2, MT):
             load_x(i, 1)
 
-        transposes(0)
-        quantise(0)
+        warm = psum.tile([P, 512], F32, tag="bank7", name="warm")
+        for d in range(WARM):
+            nc.tensor.matmul(out=warm[:], lhsT=ones[:], rhs=zeros[:], start=True, stop=True)
+
+        transposes(0, [0, 1])
+        quantise(0, [0, 1])
 
         for h in range(2):
             bank = new_bank([P, 1024], BF16)
@@ -163,8 +185,8 @@ def tile_inputscaledquantlinear_kernel(tc, x, weight_words, weight_scales, bias,
             else:
                 nc.vector.tensor_copy(out=bias_sb[:, 1024:2048], in_=bank[:])
 
-        transposes(1)
-        quantise(1)
+        transposes(1, [0, 1])
+        quantise(1, [0, 1])
 
         head = [(0, 0), (0, 512), (0, 1024), (0, 1536), (1, 0), (1, 512)]
         for (i, c0) in head:
@@ -172,34 +194,42 @@ def tile_inputscaledquantlinear_kernel(tc, x, weight_words, weight_scales, bias,
         for g in range(G):
             for (i, c0) in head:
                 mx_pass(accs[(i, c0)], i, c0, N_PASS, g)
-        transposes(2)
+        transposes(2, [0, 1])
         drain(0, 0, 512, None)
         drain(0, 512, 512, 0)
         drain(0, 1024, 512, None)
         drain(0, 1536, 512, 1024)
         drain(1, 0, 512, None)
         drain(1, 512, 512, 0)
-        quantise(2)
+        quantise(2, [0, 1])
         group(1, 1024, 512)
         group(1, 1536, 512)
-        transposes(3)
+        transposes(3, [0])
+        sort_words(4)
         drain(1, 1024, 512, None)
         drain(1, 1536, 512, 1024)
-        quantise(3)
+        quantise(3, [0])
         for i in range(2, MT):
             last = i == MT - 1
-            pieces = [(0, 512), (512, 512), (1024, 512), (1536, 512)]
-            if last:
-                step = 512 // TAPER
-                pieces = pieces[0:3] + [(1536 + step * s, step) for s in range(TAPER)]
-            for (c0, width) in pieces:
+            step = 512 // TAPER
+            end = [(1536 + step * s, step) for s in range(TAPER)] if last else [(1536, 512)]
+            group(i, 0, 512)
+            group(i, 512, 512)
+            if i + 1 < MT:
+                transposes(i + 1, [1])
+            group(i, 1024, 512)
+            for (c0, width) in end:
                 group(i, c0, width)
             if i + 2 < MT:
-                transposes(i + 2)
-            for j, (c0, width) in enumerate(pieces):
-                if last:
-                    drain(i, c0, width, c0)
-                else:
-                    drain(i, c0, width, c0 - 512 if j % 2 == 1 else None)
+                transposes(i + 2, [0])
+            if i + 3 < MT:
+                sort_words(i + 3)
+            drain(i, 0, 512, 0 if last else None)
+            drain(i, 512, 512, 512 if last else 0)
+            if i + 1 < MT:
+                quantise(i + 1, [1])
+            drain(i, 1024, 512, 1024 if last else None)
+            for (c0, width) in end:
+                drain(i, c0, width, c0 if last else 1024)
             if i + 2 < MT:
-                quantise(i + 2)
+                quantise(i + 2, [0])

@@ -86,15 +86,14 @@ def tile_inputscaledquantlinear_kernel(tc, x, weight_words, weight_scales, bias,
                 in_=x_sb[i][:].bitcast(F32).rearrange("p (g q u) -> p g u q", g=G, u=2),
             )
 
-        def transposes(i, halves):
+        def transposes(i):
             words = x_sb[i][:].bitcast(F32)
-            if halves[0] == 0:
-                grouped[i] = work.tile([P, K], BF16, name="grp", align_bytes=64)
-            grp = grouped[i]
-            banks = {}
-            for h in halves:
+            grp = work.tile([P, K], BF16, name="grp", align_bytes=64)
+            grouped[i] = grp
+            banks = []
+            for h in range(2):
                 bank = new_bank([P, 512], F32)
-                banks[h] = bank
+                banks.append(bank)
                 for s in range(4):
                     g = 2 * h + s // 2
                     u = s % 2
@@ -103,14 +102,14 @@ def tile_inputscaledquantlinear_kernel(tc, x, weight_words, weight_scales, bias,
                     else:
                         src = words[:, 256 * g + u : 256 * (g + 1) : 2]
                     nc.tensor.transpose(bank[:, P * s : P * (s + 1)], src, ident[:])
-            for h in halves:
+            for h in range(2):
                 nc.scalar.copy(
                     out=grp[:].bitcast(F32)[:, 512 * h : 512 * (h + 1)].rearrange("p (g m u) -> p g m u", g=2, u=2),
                     in_=banks[h][:].rearrange("p (g u m) -> p g m u", g=2, u=2),
                 )
 
-        def quantise(i, halves):
-            for h in halves:
+        def quantise(i):
+            for h in range(2):
                 nc.vector.quantize_mx(
                     out=xq[i][:, 256 * h : 256 * (h + 1)].bitcast(FP8X4),
                     scales=xsc[i][:, 256 * h : 256 * (h + 1)],
@@ -153,22 +152,26 @@ def tile_inputscaledquantlinear_kernel(tc, x, weight_words, weight_scales, bias,
         nc.vector.memset(wsc[1][:].rearrange("p g n -> p (g n)").bitcast(I32), 0)
         make_identity(nc, ident[:])
         load_x(0, 2)
-        load_x(1, 1)
+        load_x(1, 2)
+        load_x(2, 1)
+        load_x(3, 1)
         load_scales(0)
         load_w(0, 2)
         load_w(1, 1)
         load_scales(1)
         load_w(2, 1)
         load_w(3, 1)
-        for i in range(2, MT):
+        for i in range(4, MT):
             load_x(i, 1)
 
         warm = psum.tile([P, 512], F32, tag="bank7", name="warm")
         for d in range(WARM):
             nc.tensor.matmul(out=warm[:], lhsT=ones[:], rhs=zeros[:], start=True, stop=True)
 
-        transposes(0, [0, 1])
-        quantise(0, [0, 1])
+        transposes(0)
+        quantise(0)
+        transposes(1)
+        quantise(1)
 
         for h in range(2):
             bank = new_bank([P, 1024], BF16)
@@ -185,51 +188,36 @@ def tile_inputscaledquantlinear_kernel(tc, x, weight_words, weight_scales, bias,
             else:
                 nc.vector.tensor_copy(out=bias_sb[:, 1024:2048], in_=bank[:])
 
-        transposes(1, [0, 1])
-        quantise(1, [0, 1])
+        transposes(2)
+        transposes(3)
+        quantise(2)
+        quantise(3)
+        sort_words(4)
 
-        head = [(0, 0), (0, 512), (0, 1024), (0, 1536), (1, 0), (1, 512)]
+        head = [(i, 512 * n) for i in range(2) for n in range(NC)]
         for (i, c0) in head:
             accs[(i, c0)] = new_bank([P, 512], F32)
         for g in range(G):
             for (i, c0) in head:
                 mx_pass(accs[(i, c0)], i, c0, N_PASS, g)
-        transposes(2, [0, 1])
-        drain(0, 0, 512, None)
-        drain(0, 512, 512, 0)
-        drain(0, 1024, 512, None)
-        drain(0, 1536, 512, 1024)
-        drain(1, 0, 512, None)
-        drain(1, 512, 512, 0)
-        quantise(2, [0, 1])
-        group(1, 1024, 512)
-        group(1, 1536, 512)
-        transposes(3, [0])
-        sort_words(4)
-        drain(1, 1024, 512, None)
-        drain(1, 1536, 512, 1024)
-        quantise(3, [0])
+        for (i, c0) in head:
+            drain(i, c0, 512, c0 - 512 if c0 % 1024 == 512 else None)
         for i in range(2, MT):
             last = i == MT - 1
-            step = 512 // TAPER
-            end = [(1536 + step * s, step) for s in range(TAPER)] if last else [(1536, 512)]
-            group(i, 0, 512)
-            group(i, 512, 512)
-            if i + 1 < MT:
-                transposes(i + 1, [1])
-            group(i, 1024, 512)
-            for (c0, width) in end:
+            pieces = [(0, 512), (512, 512), (1024, 512), (1536, 512)]
+            if last:
+                step = 512 // TAPER
+                pieces = pieces[0:3] + [(1536 + step * s, step) for s in range(TAPER)]
+            for (c0, width) in pieces:
                 group(i, c0, width)
             if i + 2 < MT:
-                transposes(i + 2, [0])
+                transposes(i + 2)
             if i + 3 < MT:
                 sort_words(i + 3)
-            drain(i, 0, 512, 0 if last else None)
-            drain(i, 512, 512, 512 if last else 0)
-            if i + 1 < MT:
-                quantise(i + 1, [1])
-            drain(i, 1024, 512, 1024 if last else None)
-            for (c0, width) in end:
-                drain(i, c0, width, c0 if last else 1024)
+            for j, (c0, width) in enumerate(pieces):
+                if last:
+                    drain(i, c0, width, c0)
+                else:
+                    drain(i, c0, width, c0 - 512 if j % 2 == 1 else None)
             if i + 2 < MT:
-                quantise(i + 2, [0])
+                quantise(i + 2)

from contextlib import ExitStack

import concourse.mybir as mybir
from concourse.masks import make_identity

F32 = mybir.dt.float32
BF16 = mybir.dt.bfloat16
I32 = mybir.dt.int32
U32 = mybir.dt.uint32
U8 = mybir.dt.uint8
FP8X4 = mybir.dt.float8_e4m3fn_x4
FP4X4 = mybir.dt.float4_e2m1fn_x4
ADD = mybir.AluOpType.add

P = 128
ROWS = 1024
K = 2048
N = 2048
K_PASS = 512
N_PASS = 512
G = K // K_PASS
NC = N // N_PASS
MT = ROWS // P
FLOPS = 2 * ROWS * K * N

SORT_FROM = 4
WARM = 4
TAPER = 4


def tile_inputscaledquantlinear_kernel(tc, x, weight_words, weight_scales, bias, input_scale, out):
    nc = tc.nc
    with ExitStack() as ctx:
        keep = ctx.enter_context(tc.tile_pool(name="keep", bufs=1))
        work = ctx.enter_context(tc.tile_pool(name="work", bufs=3))
        srtp = ctx.enter_context(tc.tile_pool(name="srtp", bufs=3))
        outp = ctx.enter_context(tc.tile_pool(name="outp", bufs=4))
        psum = ctx.enter_context(tc.psum_pool(name="psum", bufs=1))
        ctx.enter_context(tc.manual_schedule())

        ident = keep.tile([P, P], F32, name="ident")
        ones = keep.tile([P, P], BF16, name="ones")
        zeros = keep.tile([P, N_PASS], BF16, name="zeros")
        brow = keep.tile([P, N], BF16, name="brow")
        bias_sb = keep.tile([P, N], BF16, name="bias_sb")
        w_sb = [keep.tile([P, 2 * N], U8, name="w%d" % g, align_bytes=64) for g in range(G)]
        wsc = [keep.tile([P, 2, N], U8, name="wsc%d" % h, align_bytes=64) for h in range(2)]
        x_sb = [keep.tile([P, K], BF16, name="x%d" % i) for i in range(MT)]
        xq = [keep.tile([P, K // 4], U32, name="xq%d" % i, align_bytes=64) for i in range(MT)]
        xsc = [keep.tile([P, K // 4], U8, name="xsc%d" % i, align_bytes=64) for i in range(MT)]

        count = [0]

        def new_bank(shape, dtype):
            b = count[0] % 8
            count[0] += 1
            return psum.tile(shape, dtype, tag="bank%d" % b, name="ps%d" % count[0])

        def load_x(i, pieces):
            step = K // pieces
            for c in range(pieces):
                cols = slice(step * c, step * (c + 1))
                nc.sync.dma_start(out=x_sb[i][:, cols], in_=x[P * i : P * (i + 1), cols])

        def load_w(g, pieces):
            step = 2 * N // pieces
            for c in range(pieces):
                cols = slice(step * c, step * (c + 1))
                nc.sync.dma_start(out=w_sb[g][:, cols].bitcast(I32), in_=weight_words[g][:, cols].bitcast(I32))

        def load_scales(h):
            for r in range(4):
                nc.sync.dma_start(
                    out=wsc[h][r:P:32, :, :].bitcast(I32),
                    in_=weight_scales[2 * h : 2 * h + 2, r:16:4, :].rearrange("g q n -> q g n").bitcast(I32),
                )

        grouped = {}
        sorted_x = {}

        def sort_words(i):
            srt = srtp.tile([P, K // 2], F32, name="srt")
            sorted_x[i] = srt
            nc.scalar.copy(
                out=srt[:].rearrange("p (g u q) -> p g u q", g=G, u=2),
                in_=x_sb[i][:].bitcast(F32).rearrange("p (g q u) -> p g u q", g=G, u=2),
            )

        def transposes(i):
            words = x_sb[i][:].bitcast(F32)
            grp = work.tile([P, K], BF16, name="grp", align_bytes=64)
            grouped[i] = grp
            banks = []
            for h in range(2):
                bank = new_bank([P, 512], F32)
                banks.append(bank)
                for s in range(4):
                    g = 2 * h + s // 2
                    u = s % 2
                    if i >= SORT_FROM:
                        src = sorted_x[i][:, P * (2 * g + u) : P * (2 * g + u + 1)]
                    else:
                        src = words[:, 256 * g + u : 256 * (g + 1) : 2]
                    nc.tensor.transpose(bank[:, P * s : P * (s + 1)], src, ident[:])
            for h in range(2):
                nc.scalar.copy(
                    out=grp[:].bitcast(F32)[:, 512 * h : 512 * (h + 1)].rearrange("p (g m u) -> p g m u", g=2, u=2),
                    in_=banks[h][:].rearrange("p (g u m) -> p g m u", g=2, u=2),
                )

        def quantise(i):
            for h in range(2):
                nc.vector.quantize_mx(
                    out=xq[i][:, 256 * h : 256 * (h + 1)].bitcast(FP8X4),
                    scales=xsc[i][:, 256 * h : 256 * (h + 1)],
                    in_=grouped[i][:, 1024 * h : 1024 * (h + 1)],
                )

        def mx_pass(acc, i, c0, width, g):
            nc.tensor.matmul_mx(
                out=acc[:, 0:width],
                lhsT=xq[i][:, P * g : P * (g + 1)].bitcast(FP8X4),
                lhsT_scale=xsc[i][:, P * g : P * (g + 1)],
                rhs=w_sb[g][:, 2 * c0 : 2 * (c0 + width)].bitcast(FP4X4),
                rhs_scale=wsc[g // 2][:, g % 2, c0 : c0 + width],
                start=(g == 0),
                stop=(g == G - 1),
            )

        accs = {}
        res = {}

        def group(i, c0, width):
            accs[(i, c0)] = new_bank([P, 512], F32)
            for g in range(G):
                mx_pass(accs[(i, c0)], i, c0, width, g)

        def drain(i, c0, width, store_from):
            if c0 == 0:
                res[i] = outp.tile([P, N], F32, name="res")
            cols = slice(c0, c0 + width)
            nc.vector.tensor_tensor(out=res[i][:, cols], in0=accs[(i, c0)][:, 0:width], in1=bias_sb[:, cols], op=ADD)
            if store_from is not None:
                c = slice(store_from, c0 + width)
                nc.sync.dma_start(out=out[P * i : P * (i + 1), c], in_=res[i][:, c])

        nc.vector.memset(ones[:], 1.0)
        nc.vector.memset(zeros[:].bitcast(I32), 0)
        nc.vector.memset(brow[:].bitcast(I32), 0)
        nc.scalar.dma_start(out=brow[0:1, :], in_=bias.rearrange("(o n) -> o n", o=1))
        nc.vector.memset(wsc[0][:].rearrange("p g n -> p (g n)").bitcast(I32), 0)
        nc.vector.memset(wsc[1][:].rearrange("p g n -> p (g n)").bitcast(I32), 0)
        make_identity(nc, ident[:])
        load_x(0, 2)
        load_x(1, 2)
        load_x(2, 1)
        load_x(3, 1)
        load_scales(0)
        load_w(0, 2)
        load_w(1, 1)
        load_scales(1)
        load_w(2, 1)
        load_w(3, 1)
        for i in range(4, MT):
            load_x(i, 1)

        warm = psum.tile([P, 512], F32, tag="bank7", name="warm")
        for d in range(WARM):
            nc.tensor.matmul(out=warm[:], lhsT=ones[:], rhs=zeros[:], start=True, stop=True)

        transposes(0)
        quantise(0)
        transposes(1)
        quantise(1)

        for h in range(2):
            bank = new_bank([P, 1024], BF16)
            for c in range(2):
                nc.tensor.matmul(
                    out=bank[:, 512 * c : 512 * (c + 1)],
                    lhsT=ones[:],
                    rhs=brow[:, 1024 * h + 512 * c : 1024 * h + 512 * (c + 1)],
                    start=True,
                    stop=True,
                )
            if h == 0:
                nc.scalar.copy(out=bias_sb[:, 0:1024], in_=bank[:])
            else:
                nc.vector.tensor_copy(out=bias_sb[:, 1024:2048], in_=bank[:])

        transposes(2)
        transposes(3)
        quantise(2)
        quantise(3)
        sort_words(4)

        head = [(i, 512 * n) for i in range(2) for n in range(NC)]
        for (i, c0) in head:
            accs[(i, c0)] = new_bank([P, 512], F32)
        for g in range(G):
            for (i, c0) in head:
                mx_pass(accs[(i, c0)], i, c0, N_PASS, g)
        for (i, c0) in head:
            drain(i, c0, 512, c0 - 512 if c0 % 1024 == 512 else None)
        for i in range(2, MT):
            last = i == MT - 1
            pieces = [(0, 512), (512, 512), (1024, 512), (1536, 512)]
            if last:
                step = 512 // TAPER
                pieces = pieces[0:3] + [(1536 + step * s, step) for s in range(TAPER)]
            for (c0, width) in pieces:
                group(i, c0, width)
            if i + 2 < MT:
                transposes(i + 2)
            if i + 3 < MT:
                sort_words(i + 3)
            for j, (c0, width) in enumerate(pieces):
                if last:
                    drain(i, c0, width, c0)
                else:
                    drain(i, c0, width, c0 - 512 if j % 2 == 1 else None)
            if i + 2 < MT:
                quantise(i + 2)
